import numpy as np
import ml_dtypes


def mxq(x, axis, fmt="e4m3"):
    dtype, down = {"e4m3": (ml_dtypes.float8_e4m3fn, 7), "e5m2": (ml_dtypes.float8_e5m2, 14)}[fmt]
    v = np.moveaxis(np.asarray(x, np.float32).astype(ml_dtypes.bfloat16).astype(np.float64), axis, -1)
    blocks = v.reshape(v.shape[:-1] + (-1, 32))
    amax = np.abs(blocks).max(-1, keepdims=True)
    byte = np.maximum(np.where(amax > 0, np.frexp(amax)[1] - 1 + 127, 0) - down, 1)
    scale = np.exp2(byte - 127.0)
    codes = (blocks / scale).astype(np.float32).astype(dtype).astype(np.float64)
    return np.moveaxis((codes * scale).reshape(v.shape), -1, axis)


WIDE = False


def mx_kscale(k):
    if not WIDE:
        return np.ones(k)
    levels = np.array([10, -10, 5, -5, 0])
    if k % 512:
        return np.exp2(np.random.permutation(np.resize(levels, k // 32))).repeat(32)
    a = np.empty((k // 512, 16))
    for p in range(k // 512):
        a[p, :8] = np.random.permutation(np.resize(levels, 8))
        for g in range(8):
            far = levels[np.abs(levels - a[p, g]) >= 10]
            a[p, g + 8] = far[np.random.randint(len(far))]
    return np.exp2(a.ravel()).repeat(32)


BF16 = ml_dtypes.bfloat16


def bf(x):
    return np.asarray(x, np.float32).astype(BF16)


def f64(x):
    return np.asarray(x).astype(np.float64)


B, N, C, DIM, H = 4, 128, 2048, 2048, 16
D = DIM // H // 2
LAYER_NUM = 12
LAM_INIT = 0.8 - 0.6 * np.exp(-0.3 * LAYER_NUM)
SCALE = D ** -0.5


def split_qk(y):
    y = y.reshape(B, N, H, D, 2)
    return np.moveaxis(y, -1, 2).reshape(B, N, 2 * H, D)


def setup_inputs():
    s = mx_kscale(C)
    ls = 0.45 / D ** 0.25
    return {"x": bf(np.random.standard_normal((B, N, C)) * s),
            "Wq": bf(np.random.standard_normal((DIM, C)) / np.sqrt(C) / s),
            "Wk": bf(np.random.standard_normal((DIM, C)) / np.sqrt(C) / s),
            "lq1": bf(np.random.standard_normal(D) * ls),
            "lq2": bf(np.random.standard_normal(D) * ls),
            "lk1": bf(np.random.standard_normal(D) * ls),
            "lk2": bf(np.random.standard_normal(D) * ls)}


def reference(x, Wq, Wk, lq1, lq2, lk1, lk2):
    xq = mxq(f64(x), 2, "e4m3")
    q = split_qk(xq @ mxq(f64(Wq), 1, "e4m3").T) * SCALE
    k = split_qk(xq @ mxq(f64(Wk), 1, "e4m3").T)
    sc = np.stack([(q[:, :, i:i + 1, :] * k).sum(-1) for i in range(2 * H)], axis=2)
    e = np.exp(sc - sc.max(-1, keepdims=True))
    att = e / e.sum(-1, keepdims=True)
    lam = np.exp(np.sum(f64(lq1) * f64(lk1))) - np.exp(np.sum(f64(lq2) * f64(lk2))) + LAM_INIT
    return att[:, :, :H, :H] - lam * att[:, :, H:, H:]

@@ -1,0 +1,287 @@
+import math
+
+import concourse.mybir as mybir
+from concourse.masks import make_identity
+
+F32 = mybir.dt.float32
+BF16 = mybir.dt.bfloat16
+U32 = mybir.dt.uint32
+U8 = mybir.dt.uint8
+FP8X4 = mybir.dt.float8_e4m3fn_x4
+ALU = mybir.AluOpType
+ACT = mybir.ActivationFunctionType
+AXIS_X = mybir.AxisListType.X
+
+P = 128
+PACK = 4
+K_PASS = P * PACK
+TOKENS = 512
+C = 2048
+DIM = 2048
+H = 16
+D = 64
+HEAD_ROWS = 2 * H
+PASSES = C // K_PASS
+CHUNK = 512
+ROW_TILES = CHUNK // P
+CHUNKS_PER_W = DIM // CHUNK
+HEADS_PER_CHUNK = CHUNK // (2 * D)
+WORDS = P
+SLOTS = TOKENS // 2
+GROUPS = SLOTS // 2
+BATCH = 8
+BATCHES = GROUPS // BATCH
+SOFT_STAGES = 7
+SCALE = D ** -0.5
+LAM_INIT = 0.8 - 0.6 * math.exp(-0.3 * 12)
+
+FLOPS = 2 * TOKENS * C * DIM * 2 + 2 * TOKENS * HEAD_ROWS * HEAD_ROWS * D
+
+
+def tile_differentialattention_pa_kernel(tc, x, Wq, Wk, lq1, lq2, lk1, lk2, out):
+    nc = tc.nc
+
+    x_rows = x.rearrange("b n c -> (b n) c").rearrange("(pr r t) c -> pr r t c", pr=2, t=2)
+    out_rows = out.rearrange("b n a h -> (b n a) h").rearrange("(w u r) h -> u r w h", u=2, r=2 * H)
+
+    with tc.manual_schedule(), tc.tile_pool(name="const", bufs=1) as const, tc.tile_pool(
+        name="heads", bufs=1
+    ) as heads, tc.psum_pool(name="turned", bufs=4) as turned, tc.psum_pool(name="sums", bufs=4) as sums:
+        ident = const.tile([P, P], F32)
+        make_identity(nc, ident[:])
+
+        q_cols = heads.tile([P, SLOTS, 2 * HEAD_ROWS], F32)
+        k_cols = heads.tile([P, SLOTS, HEAD_ROWS], F32)
+        for piece in range(16):
+            nc.gpsimd.memset(q_cols[:, 16 * piece : 16 * piece + 16, :], 0.0)
+
+        shift_up = const.tile([P, 2, 2, 2 * H], F32)
+        nc.vector.memset(shift_up[:], 0.0)
+        nc.vector.tensor_copy(out=shift_up[:, :, 0, :], in_=ident[:].rearrange("p (u j r) -> p u j r", u=2, j=2)[:, :, 1, :])
+
+        vectors = const.tile([P, 4, D], BF16)
+        for i, vec in enumerate((lq1, lq2, lk1, lk2)):
+            nc.scalar.dma_start(out=vectors[:, i, :], in_=vec.partition_broadcast(P))
+        with tc.tile_pool(name="raw", bufs=3) as raw_pool, tc.tile_pool(name="grouped", bufs=2) as grouped_pool, tc.tile_pool(
+            name="wq", bufs=2
+        ) as w_pool, tc.tile_pool(name="xq", bufs=1) as x_pool, tc.tile_pool(name="y", bufs=2) as y_pool:
+
+            def new_grouped():
+                grouped = grouped_pool.tile([P, PASSES, PACK * CHUNK], BF16, align_bytes=64)
+                return grouped
+
+            def turn_row_tile(raw, grouped, r):
+                raw_words = raw[:].bitcast(F32)
+                grouped_words = grouped[:].bitcast(F32).rearrange("p g (o u) -> p g o u", u=2)
+                for pair in range(PASSES // 2):
+                    bank = turned.tile([P, 2, 2, P], F32, tag="turned")
+                    for g in range(2):
+                        for u in range(2):
+                            first = 2 * WORDS * (2 * pair + g) + u
+                            nc.tensor.transpose(
+                                out=bank[:, g, u, :], in_=raw_words[:, r, first : first + 2 * WORDS - 1 : 2], identity=ident[:]
+                            )
+                    copy = nc.scalar.copy if pair == 0 else nc.vector.tensor_copy
+                    copy(
+                        out=grouped_words[:, 2 * pair : 2 * pair + 2, P * r : P * r + P, :],
+                        in_=bank[:].rearrange("p g u o -> p g o u"),
+                    )
+
+            def quantise(grouped, codes, scales):
+                for g in range(PASSES):
+                    nc.vector.quantize_mx(
+                        out=codes[:, g, :].bitcast(FP8X4), scales=scales[:, g, :], in_=grouped[:, g, :]
+                    )
+
+            def project_tile(w_codes, w_scales, y, t):
+                tokens = slice(P * t, P * t + P)
+                acc = sums.tile([P, CHUNK], F32, tag="sums")
+                for g in range(PASSES):
+                    nc.tensor.matmul_mx(
+                        out=acc[:],
+                        lhsT=x_codes[:, g, tokens].bitcast(FP8X4),
+                        lhsT_scale=x_scales[:, g, tokens],
+                        rhs=w_codes[:, g, :].bitcast(FP8X4),
+                        rhs_scale=w_scales[:, g, :],
+                        start=(g == 0),
+                        stop=(g == PASSES - 1),
+                    )
+                nc.scalar.copy(
+                    out=y[:, :, :, t, :], in_=acc[:].rearrange("p (h d j) -> p j h d", h=HEADS_PER_CHUNK, j=2)
+                )
+
+            def turn_heads(y, n, is_q, first_head):
+                pr, j = n // 2, n % 2
+                bank = turned.tile([P, HEADS_PER_CHUNK, P], F32, tag="turned")
+                for h in range(HEADS_PER_CHUNK):
+                    nc.tensor.transpose(
+                        out=bank[:, h, :],
+                        in_=y[:, j, h, 2 * pr : 2 * pr + 2, :].rearrange("p t d -> p (t d)"),
+                        identity=ident[:],
+                    )
+                by_slot = bank[:].rearrange("p h s -> p s h")
+                slots = slice(P * pr, P * pr + P)
+                copy = nc.vector.tensor_copy if n % 2 == 0 else nc.scalar.copy
+                if is_q:
+                    for t in range(2):
+                        rows = slice(D * t, D * t + D)
+                        col = 2 * H * j + H * t + first_head
+                        copy(out=q_cols[rows, slots, col : col + HEADS_PER_CHUNK], in_=by_slot[rows])
+                else:
+                    col = H * j + first_head
+                    copy(out=k_cols[:, slots, col : col + HEADS_PER_CHUNK], in_=by_slot)
+
+            def load_w(c):
+                w = Wk if c < CHUNKS_PER_W else Wq
+                first = CHUNK * (c % CHUNKS_PER_W)
+                raw = raw_pool.tile([P, ROW_TILES, C], BF16, tag="raw")
+                for r in range(ROW_TILES):
+                    nc.sync.dma_start(out=raw[:, r, :], in_=w[first + P * r : first + P * r + P, :])
+                return raw
+
+            def new_w_codes():
+                codes = w_pool.tile([P, PASSES, CHUNK], U32, align_bytes=64, tag="w_codes")
+                scales = w_pool.tile([P, PASSES, CHUNK], U8, align_bytes=64, tag="w_scales")
+                return codes, scales
+
+            n_chunks = 2 * CHUNKS_PER_W
+            x_raw = raw_pool.tile([P, ROW_TILES, C], BF16, tag="raw")
+            for pr in range(2):
+                for t in range(2):
+                    nc.sync.dma_start(out=x_raw[:, 2 * pr + t, :], in_=x_rows[pr][:, t, :])
+            raws = {0: load_w(0), 1: load_w(1)}
+
+            x_codes = x_pool.tile([P, PASSES, TOKENS], U32, align_bytes=64)
+            x_scales = x_pool.tile([P, PASSES, TOKENS], U8, align_bytes=64)
+            x_grouped = new_grouped()
+            for r in range(ROW_TILES):
+                turn_row_tile(x_raw, x_grouped, r)
+            quantise(x_grouped, x_codes, x_scales)
+
+            groupeds = {0: new_grouped()}
+            for r in range(ROW_TILES):
+                turn_row_tile(raws[0], groupeds[0], r)
+            ready = {0: new_w_codes()}
+            quantise(groupeds[0], ready[0][0], ready[0][1])
+
+            products = const.tile([P, 2, D], F32)
+            nc.vector.tensor_tensor(out=products[:], in0=vectors[:, 0:2, :], in1=vectors[:, 2:4, :], op=ALU.mult)
+            dots = const.tile([P, 2], F32)
+            nc.vector.tensor_reduce(out=dots[:], in_=products[:], axis=AXIS_X, op=ALU.add)
+            exps = const.tile([P, 2], F32)
+            nc.scalar.activation(out=exps[:], in_=dots[:], func=ACT.Exp)
+
+            ys = {}
+            for c in range(n_chunks):
+                if c + 2 < n_chunks:
+                    raws[c + 2] = load_w(c + 2)
+                if c + 1 < n_chunks:
+                    groupeds[c + 1] = new_grouped()
+                ys[c] = y_pool.tile([P, 2, HEADS_PER_CHUNK, ROW_TILES, D], F32, tag="y", name="y")
+                for t in range(ROW_TILES):
+                    if c + 1 < n_chunks:
+                        turn_row_tile(raws[c + 1], groupeds[c + 1], t)
+                    if c + 1 < n_chunks and t == ROW_TILES - 1:
+                        ready[c + 1] = new_w_codes()
+                        quantise(groupeds[c + 1], ready[c + 1][0], ready[c + 1][1])
+                    if c >= 1:
+                        turn_heads(ys[c - 1], t, c - 1 >= CHUNKS_PER_W, HEADS_PER_CHUNK * ((c - 1) % CHUNKS_PER_W))
+                    project_tile(ready[c][0], ready[c][1], ys[c], t)
+            neg_lam = const.tile([P, 1], F32)
+            nc.vector.tensor_scalar(
+                out=neg_lam[:], in0=exps[:, 1:2], scalar1=exps[:, 0:1], scalar2=-LAM_INIT, op0=ALU.subtract, op1=ALU.add
+            )
+            nc.vector.tensor_scalar(out=shift_up[:], in0=shift_up[:], scalar1=neg_lam[:, 0:1], scalar2=None, op0=ALU.mult)
+
+            for n in range(4):
+                turn_heads(ys[n_chunks - 1], n, True, HEADS_PER_CHUNK * (CHUNKS_PER_W - 1))
+
+        with tc.tile_pool(name="soft", bufs=SOFT_STAGES + 1) as soft, tc.tile_pool(name="stats", bufs=SOFT_STAGES + 1) as stats:
+            wide = [P, BATCH, HEAD_ROWS]
+            banks, atts, tops, totals, inverses, moveds = {}, {}, {}, {}, {}, {}
+
+            def scores(b):
+                banks[b] = sums.tile([P, BATCH, 2 * HEAD_ROWS], F32, tag="sums", name="bank")
+                for i in range(BATCH):
+                    w = BATCH * b + i
+                    nc.tensor.matmul(
+                        out=banks[b][:, i, :],
+                        lhsT=q_cols[:, 2 * w : 2 * w + 2, :].rearrange("p s c -> p (s c)"),
+                        rhs=k_cols[:, 2 * w : 2 * w + 2, :].rearrange("p s c -> p (s c)"),
+                        start=True,
+                        stop=True,
+                    )
+
+            def copy_scores(b):
+                atts[b] = soft.tile(wide, F32, tag="att", name="att")
+                for u in range(2):
+                    rows = slice(D * u, D * u + D)
+                    nc.scalar.copy(out=atts[b][rows], in_=banks[b][rows, :, HEAD_ROWS * u : HEAD_ROWS * (u + 1)])
+
+            def largest(b):
+                tops[b] = stats.tile([P, BATCH], F32, tag="top", name="top")
+                nc.vector.tensor_reduce(out=tops[b][:], in_=atts[b][:], axis=AXIS_X, op=ALU.max)
+
+            def shift(b):
+                nc.vector.tensor_tensor(
+                    out=atts[b][:], in0=atts[b][:], in1=tops[b][:].unsqueeze(2).to_broadcast(wide), op=ALU.subtract
+                )
+
+            def exponential(b):
+                nc.scalar.activation(out=atts[b][:], in_=atts[b][:], func=ACT.Exp, scale=SCALE)
+
+            def add_up(b):
+                totals[b] = stats.tile([P, BATCH], F32, tag="total", name="total")
+                nc.vector.tensor_reduce(out=totals[b][:], in_=atts[b][:], axis=AXIS_X, op=ALU.add)
+
+            def invert(b):
+                inverses[b] = stats.tile([P, BATCH], F32, tag="inverse", name="inverse")
+                nc.vector.reciprocal(out=inverses[b][:], in_=totals[b][:])
+
+            def divide(b):
+                nc.vector.tensor_tensor(
+                    out=atts[b][:], in0=atts[b][:], in1=inverses[b][:].unsqueeze(2).to_broadcast(wide), op=ALU.mult
+                )
+
+            def move_up(b):
+                moveds[b] = turned.tile([P, BATCH, H], F32, tag="turned", name="moved")
+                nc.tensor.matmul(
+                    out=moveds[b][:],
+                    lhsT=shift_up[:].rearrange("p u j r -> p (u j r)"),
+                    rhs=atts[b][:, :, H : 2 * H],
+                    start=True,
+                    stop=True,
+                )
+
+            def difference(b):
+                result = soft.tile([P, BATCH, H], F32, tag="result")
+                nc.vector.tensor_tensor(out=result[:], in0=atts[b][:, :, 0:H], in1=moveds[b][:], op=ALU.add)
+                for u in range(2):
+                    nc.sync.dma_start(
+                        out=out_rows[u][:, BATCH * b : BATCH * (b + 1), :], in_=result[D * u : D * u + 2 * H]
+                    )
+
+            def live(b):
+                return 0 <= b < BATCHES
+
+            for r in range(BATCHES + SOFT_STAGES - 1):
+                if live(r):
+                    scores(r)
+                if live(r - 5):
+                    move_up(r - 5)
+                if live(r - 1):
+                    copy_scores(r - 1)
+                if live(r - 3):
+                    exponential(r - 3)
+                if live(r - 2):
+                    largest(r - 2)
+                if live(r - 4):
+                    add_up(r - 4)
+                if live(r - 2):
+                    shift(r - 2)
+                if live(r - 4):
+                    invert(r - 4)
+                if live(r - 6):
+                    difference(r - 6)
+                if live(r - 4):
+                    divide(r - 4)

@@ -55,9 +55,6 @@ def tile_differentialattention_pa_kernel(tc, x, Wq, Wk, lq1, lq2, lk1, lk2, out)
         for piece in range(16):
             nc.gpsimd.memset(q_cols[:, 16 * piece : 16 * piece + 16, :], 0.0)
 
-        shift_up = const.tile([P, 2, 2, 2 * H], F32)
-        nc.vector.memset(shift_up[:], 0.0)
-        nc.vector.tensor_copy(out=shift_up[:, :, 0, :], in_=ident[:].rearrange("p (u j r) -> p u j r", u=2, j=2)[:, :, 1, :])
 
         vectors = const.tile([P, 4, D], BF16)
         for i, vec in enumerate((lq1, lq2, lk1, lk2)):
@@ -191,7 +188,6 @@ def tile_differentialattention_pa_kernel(tc, x, Wq, Wk, lq1, lq2, lk1, lk2, out)
             nc.vector.tensor_scalar(
                 out=neg_lam[:], in0=exps[:, 1:2], scalar1=exps[:, 0:1], scalar2=-LAM_INIT, op0=ALU.subtract, op1=ALU.add
             )
-            nc.vector.tensor_scalar(out=shift_up[:], in0=shift_up[:], scalar1=neg_lam[:, 0:1], scalar2=None, op0=ALU.mult)
 
             for n in range(4):
                 turn_heads(ys[n_chunks - 1], n, True, HEADS_PER_CHUNK * (CHUNKS_PER_W - 1))
@@ -244,22 +240,25 @@ def tile_differentialattention_pa_kernel(tc, x, Wq, Wk, lq1, lq2, lk1, lk2, out)
                 )
 
             def move_up(b):
-                moveds[b] = turned.tile([P, BATCH, H], F32, tag="turned", name="moved")
-                nc.tensor.matmul(
-                    out=moveds[b][:],
-                    lhsT=shift_up[:].rearrange("p u j r -> p (u j r)"),
-                    rhs=atts[b][:, :, H : 2 * H],
-                    start=True,
-                    stop=True,
-                )
+                moveds[b] = soft.tile([P, BATCH, H], F32, tag="moved", name="moved")
+                for u in range(2):
+                    nc.sync.dma_start(
+                        out=moveds[b][D * u : D * u + 2 * H], in_=atts[b][D * u + 2 * H : D * u + 4 * H, :, H : 2 * H]
+                    )
 
             def difference(b):
                 result = soft.tile([P, BATCH, H], F32, tag="result")
-                nc.vector.tensor_tensor(out=result[:], in0=atts[b][:, :, 0:H], in1=moveds[b][:], op=ALU.add)
                 for u in range(2):
-                    nc.sync.dma_start(
-                        out=out_rows[u][:, BATCH * b : BATCH * (b + 1), :], in_=result[D * u : D * u + 2 * H]
+                    rows = slice(D * u, D * u + 2 * H)
+                    nc.vector.scalar_tensor_tensor(
+                        out=result[rows],
+                        in0=moveds[b][rows],
+                        scalar=neg_lam[rows, 0:1],
+                        in1=atts[b][rows, :, 0:H],
+                        op0=ALU.mult,
+                        op1=ALU.add,
                     )
+                    nc.sync.dma_start(out=out_rows[u][:, BATCH * b : BATCH * (b + 1), :], in_=result[rows])
 
             def live(b):
                 return 0 <= b < BATCHES
@@ -267,8 +266,6 @@ def tile_differentialattention_pa_kernel(tc, x, Wq, Wk, lq1, lq2, lk1, lk2, out)
             for r in range(BATCHES + SOFT_STAGES - 1):
                 if live(r):
                     scores(r)
-                if live(r - 5):
-                    move_up(r - 5)
                 if live(r - 1):
                     copy_scores(r - 1)
                 if live(r - 3):
@@ -285,3 +282,4 @@ def tile_differentialattention_pa_kernel(tc, x, Wq, Wk, lq1, lq2, lk1, lk2, out)
                     difference(r - 6)
                 if live(r - 4):
                     divide(r - 4)
+                    move_up(r - 4)

@@ -22,12 +22,13 @@ H = 16
 D = 64
 HEAD_ROWS = 2 * H
 PASSES = C // K_PASS
-CHUNK = 512
-ROW_TILES = CHUNK // P
-CHUNKS_PER_W = DIM // CHUNK
-HEADS_PER_CHUNK = CHUNK // (2 * D)
 WORDS = P
 SLOTS = TOKENS // 2
+X_TILES = TOKENS // P
+TILES = X_TILES + 2 * H
+HEADS = 4
+STEP = 2
+HELD = 2 * HEADS
 GROUPS = SLOTS // 2
 BATCH = 8
 BATCHES = GROUPS // BATCH
@@ -41,7 +42,7 @@ FLOPS = 2 * TOKENS * C * DIM * 2 + 2 * TOKENS * HEAD_ROWS * HEAD_ROWS * D
 def tile_differentialattention_pa_kernel(tc, x, Wq, Wk, lq1, lq2, lk1, lk2, out):
     nc = tc.nc
 
-    x_rows = x.rearrange("b n c -> (b n) c").rearrange("(pr r t) c -> pr r t c", pr=2, t=2)
+    x_rows = x.rearrange("b n c -> (b n) c").rearrange("(v s t) c -> v t s c", v=2, t=2)
     out_rows = out.rearrange("b n a h -> (b n a) h").rearrange("(w u r) h -> u r w h", u=2, r=2 * H)
 
     with tc.manual_schedule(), tc.tile_pool(name="const", bufs=1) as const, tc.tile_pool(
@@ -49,155 +50,208 @@ def tile_differentialattention_pa_kernel(tc, x, Wq, Wk, lq1, lq2, lk1, lk2, out)
     ) as heads, tc.psum_pool(name="turned", bufs=4) as turned, tc.psum_pool(name="sums", bufs=4) as sums:
         ident = const.tile([P, P], F32)
         make_identity(nc, ident[:])
+        by_half = const.tile([P, P], F32)
+        nc.vector.tensor_copy(
+            out=by_half[:].rearrange("p (j d) -> p j d", j=2), in_=ident[:].rearrange("p (d j) -> p j d", j=2)
+        )
 
         q_cols = heads.tile([P, SLOTS, 2 * HEAD_ROWS], F32)
         k_cols = heads.tile([P, SLOTS, HEAD_ROWS], F32)
         for piece in range(16):
             nc.gpsimd.memset(q_cols[:, 16 * piece : 16 * piece + 16, :], 0.0)
 
-
         vectors = const.tile([P, 4, D], BF16)
         for i, vec in enumerate((lq1, lq2, lk1, lk2)):
             nc.scalar.dma_start(out=vectors[:, i, :], in_=vec.partition_broadcast(P))
-        with tc.tile_pool(name="raw", bufs=3) as raw_pool, tc.tile_pool(name="grouped", bufs=2) as grouped_pool, tc.tile_pool(
-            name="wq", bufs=2
-        ) as w_pool, tc.tile_pool(name="xq", bufs=1) as x_pool, tc.tile_pool(name="y", bufs=2) as y_pool:
+        exps = const.tile([P, 2], F32)
+        neg_lam = const.tile([P, 1], F32)
 
-            def new_grouped():
-                grouped = grouped_pool.tile([P, PASSES, PACK * CHUNK], BF16, align_bytes=64)
-                return grouped
+        with tc.tile_pool(name="raw", bufs=3 * STEP) as raw_pool, tc.tile_pool(
+            name="grouped", bufs=2 * STEP
+        ) as grouped_pool, tc.tile_pool(name="wq", bufs=HELD + STEP) as w_pool, tc.tile_pool(
+            name="xq", bufs=1
+        ) as x_pool, tc.tile_pool(name="y", bufs=2) as y_pool, tc.tile_pool(name="soft", bufs=SOFT_STAGES + 1) as soft, tc.tile_pool(
+            name="stats", bufs=SOFT_STAGES + 1
+        ) as stats:
+            x_codes = x_pool.tile([P, PASSES, TOKENS], U32, align_bytes=64)
+            x_scales = x_pool.tile([P, PASSES, TOKENS], U8, align_bytes=64)
+            raws, turneds, groupeds, codes, accs, kepts, crossed = {}, {}, {}, {}, {}, {}, {}
 
-            def turn_row_tile(raw, grouped, r):
-                raw_words = raw[:].bitcast(F32)
-                grouped_words = grouped[:].bitcast(F32).rearrange("p g (o u) -> p g o u", u=2)
+            def load(n):
+                raws[n] = raw_pool.tile([P, C], BF16, tag="raw", name="raw")
+                if n < X_TILES:
+                    rows = x_rows[n // 2][n % 2]
+                else:
+                    i = n - X_TILES
+                    rows = (Wk, Wq)[i // H][P * (i % H) : P * (i % H) + P, :]
+                nc.sync.dma_start(out=raws[n][:], in_=rows)
+
+            def turn(n):
+                words = raws[n][:].bitcast(F32)
+                turneds[n] = []
                 for pair in range(PASSES // 2):
-                    bank = turned.tile([P, 2, 2, P], F32, tag="turned")
+                    bank = turned.tile([P, 2, 2, P], F32, tag="turned", name="turned_bank")
                     for g in range(2):
                         for u in range(2):
                             first = 2 * WORDS * (2 * pair + g) + u
                             nc.tensor.transpose(
-                                out=bank[:, g, u, :], in_=raw_words[:, r, first : first + 2 * WORDS - 1 : 2], identity=ident[:]
+                                out=bank[:, g, u, :],
+                                in_=words[:, first : first + 2 * WORDS - 1 : 2],
+                                identity=(ident if n < X_TILES else by_half)[:],
                             )
-                    copy = nc.scalar.copy if pair == 0 else nc.vector.tensor_copy
-                    copy(
-                        out=grouped_words[:, 2 * pair : 2 * pair + 2, P * r : P * r + P, :],
-                        in_=bank[:].rearrange("p g u o -> p g o u"),
-                    )
+                    turneds[n].append(bank)
 
-            def quantise(grouped, codes, scales):
-                for g in range(PASSES):
-                    nc.vector.quantize_mx(
-                        out=codes[:, g, :].bitcast(FP8X4), scales=scales[:, g, :], in_=grouped[:, g, :]
-                    )
-
-            def project_tile(w_codes, w_scales, y, t):
-                tokens = slice(P * t, P * t + P)
-                acc = sums.tile([P, CHUNK], F32, tag="sums")
-                for g in range(PASSES):
-                    nc.tensor.matmul_mx(
-                        out=acc[:],
-                        lhsT=x_codes[:, g, tokens].bitcast(FP8X4),
-                        lhsT_scale=x_scales[:, g, tokens],
-                        rhs=w_codes[:, g, :].bitcast(FP8X4),
-                        rhs_scale=w_scales[:, g, :],
-                        start=(g == 0),
-                        stop=(g == PASSES - 1),
-                    )
-                nc.scalar.copy(
-                    out=y[:, :, :, t, :], in_=acc[:].rearrange("p (h d j) -> p j h d", h=HEADS_PER_CHUNK, j=2)
+            def lift(n, pair, copy):
+                if pair == 0:
+                    groupeds[n] = grouped_pool.tile([P, PASSES, PACK * P], BF16, align_bytes=64, tag="grouped", name="grouped")
+                grouped_words = groupeds[n][:].bitcast(F32).rearrange("p g (o u) -> p g o u", u=2)
+                copy(
+                    out=grouped_words[:, 2 * pair : 2 * pair + 2], in_=turneds[n][pair][:].rearrange("p g u o -> p g o u")
                 )
 
-            def turn_heads(y, n, is_q, first_head):
-                pr, j = n // 2, n % 2
-                bank = turned.tile([P, HEADS_PER_CHUNK, P], F32, tag="turned")
-                for h in range(HEADS_PER_CHUNK):
-                    nc.tensor.transpose(
-                        out=bank[:, h, :],
-                        in_=y[:, j, h, 2 * pr : 2 * pr + 2, :].rearrange("p t d -> p (t d)"),
-                        identity=ident[:],
-                    )
-                by_slot = bank[:].rearrange("p h s -> p s h")
-                slots = slice(P * pr, P * pr + P)
-                copy = nc.vector.tensor_copy if n % 2 == 0 else nc.scalar.copy
-                if is_q:
-                    for t in range(2):
-                        rows = slice(D * t, D * t + D)
-                        col = 2 * H * j + H * t + first_head
-                        copy(out=q_cols[rows, slots, col : col + HEADS_PER_CHUNK], in_=by_slot[rows])
+            def quantise(n):
+                if n < X_TILES:
+                    tokens = slice(P * n, P * n + P)
+                    for g in range(PASSES):
+                        nc.vector.quantize_mx(
+                            out=x_codes[:, g, tokens].bitcast(FP8X4), scales=x_scales[:, g, tokens], in_=groupeds[n][:, g, :]
+                        )
                 else:
-                    col = H * j + first_head
-                    copy(out=k_cols[:, slots, col : col + HEADS_PER_CHUNK], in_=by_slot)
+                    w_codes = w_pool.tile([P, PASSES * P], U32, align_bytes=64, tag="w_codes", name="w_codes")
+                    w_scales = w_pool.tile([P, PASSES * P], U8, align_bytes=64, tag="w_scales", name="w_scales")
+                    nc.vector.quantize_mx(
+                        out=w_codes[:].bitcast(FP8X4), scales=w_scales[:], in_=groupeds[n][:].rearrange("p g w -> p (g w)")
+                    )
+                    codes[n] = (w_codes, w_scales)
 
-            def load_w(c):
-                w = Wk if c < CHUNKS_PER_W else Wq
-                first = CHUNK * (c % CHUNKS_PER_W)
-                raw = raw_pool.tile([P, ROW_TILES, C], BF16, tag="raw")
-                for r in range(ROW_TILES):
-                    nc.sync.dma_start(out=raw[:, r, :], in_=w[first + P * r : first + P * r + P, :])
-                return raw
+            def multiply(ns, v):
+                acc = sums.tile([P, len(ns), TOKENS // len(ns)], F32, tag="sums", name="acc")
+                tokens = slice(0, TOKENS) if v is None else slice(TOKENS // 2 * v, TOKENS // 2 * (v + 1))
+                for i, n in enumerate(ns):
+                    w_codes, w_scales = codes[n]
+                    for g in range(PASSES):
+                        rows = slice(P * g, P * g + P)
+                        nc.tensor.matmul_mx(
+                            out=acc[:, i, :],
+                            lhsT=w_codes[:, rows].bitcast(FP8X4),
+                            lhsT_scale=w_scales[:, rows],
+                            rhs=x_codes[:, g, tokens].bitcast(FP8X4),
+                            rhs_scale=x_scales[:, g, tokens],
+                            start=(g == 0),
+                            stop=(g == PASSES - 1),
+                        )
+                accs[ns[0], v] = acc
 
-            def new_w_codes():
-                codes = w_pool.tile([P, PASSES, CHUNK], U32, align_bytes=64, tag="w_codes")
-                scales = w_pool.tile([P, PASSES, CHUNK], U8, align_bytes=64, tag="w_scales")
-                return codes, scales
+            def halves(v):
+                return slice(0, 2) if v is None else slice(v, v + 1)
 
-            n_chunks = 2 * CHUNKS_PER_W
-            x_raw = raw_pool.tile([P, ROW_TILES, C], BF16, tag="raw")
-            for pr in range(2):
+            def keep(ns, v):
+                b, h = divmod(ns[0] - X_TILES, HEADS)
+                if b not in kepts:
+                    kepts[b] = y_pool.tile([P, HEADS, 2, 2, P], F32, tag="kept", name="kept")
+                    crossed[b] = y_pool.tile([P, HEADS, 2, P], F32, tag="crossed", name="crossed")
+                nc.scalar.copy(
+                    out=kepts[b][:, h : h + len(ns), halves(v)].rearrange("p h v t s -> p h (v t s)"), in_=accs[ns[0], v][:]
+                )
+
+            def cross(b, v):
                 for t in range(2):
-                    nc.sync.dma_start(out=x_raw[:, 2 * pr + t, :], in_=x_rows[pr][:, t, :])
-            raws = {0: load_w(0), 1: load_w(1)}
+                    to = slice(D * t, D * t + D)
+                    come = slice(D * (1 - t), D * (1 - t) + D)
+                    nc.sync.dma_start(out=crossed[b][to, :, halves(v)], in_=kepts[b][come, :, halves(v), t, :])
 
-            x_codes = x_pool.tile([P, PASSES, TOKENS], U32, align_bytes=64)
-            x_scales = x_pool.tile([P, PASSES, TOKENS], U8, align_bytes=64)
-            x_grouped = new_grouped()
-            for r in range(ROW_TILES):
-                turn_row_tile(x_raw, x_grouped, r)
-            quantise(x_grouped, x_codes, x_scales)
+            def place(b, quarter, v):
+                t = quarter % 2
+                rows = slice(D * t, D * t + D)
+                if quarter < 2:
+                    j = t
+                    source = kepts[b][rows, :, halves(v), t, :]
+                else:
+                    j = 1 - t
+                    source = crossed[b][rows, :, halves(v)]
+                first = HEADS * (b % (H // HEADS))
+                if b < H // HEADS:
+                    cols, col = k_cols, H * j + first
+                else:
+                    cols, col = q_cols, 2 * H * j + H * t + first
+                nc.vector.tensor_copy(
+                    out=cols[rows, :, col : col + HEADS].rearrange("p (v s) h -> p v s h", v=2)[:, halves(v)],
+                    in_=source.rearrange("p h v s -> p v s h"),
+                )
 
-            groupeds = {0: new_grouped()}
-            for r in range(ROW_TILES):
-                turn_row_tile(raws[0], groupeds[0], r)
-            ready = {0: new_w_codes()}
-            quantise(groupeds[0], ready[0][0], ready[0][1])
+            def tiles_of(step):
+                return [n for n in range(STEP * step, STEP * step + STEP) if 0 <= n < TILES]
 
-            products = const.tile([P, 2, D], F32)
-            nc.vector.tensor_tensor(out=products[:], in0=vectors[:, 0:2, :], in1=vectors[:, 2:4, :], op=ALU.mult)
-            dots = const.tile([P, 2], F32)
-            nc.vector.tensor_reduce(out=dots[:], in_=products[:], axis=AXIS_X, op=ALU.add)
-            exps = const.tile([P, 2], F32)
-            nc.scalar.activation(out=exps[:], in_=dots[:], func=ACT.Exp)
+            def w_tiles_of(step):
+                return [n for n in tiles_of(step) if n >= X_TILES]
 
-            ys = {}
-            for c in range(n_chunks):
-                if c + 2 < n_chunks:
-                    raws[c + 2] = load_w(c + 2)
-                if c + 1 < n_chunks:
-                    groupeds[c + 1] = new_grouped()
-                ys[c] = y_pool.tile([P, 2, HEADS_PER_CHUNK, ROW_TILES, D], F32, tag="y", name="y")
-                for t in range(ROW_TILES):
-                    if c + 1 < n_chunks:
-                        turn_row_tile(raws[c + 1], groupeds[c + 1], t)
-                    if c + 1 < n_chunks and t == ROW_TILES - 1:
-                        ready[c + 1] = new_w_codes()
-                        quantise(groupeds[c + 1], ready[c + 1][0], ready[c + 1][1])
-                    if c >= 1:
-                        turn_heads(ys[c - 1], t, c - 1 >= CHUNKS_PER_W, HEADS_PER_CHUNK * ((c - 1) % CHUNKS_PER_W))
-                    project_tile(ready[c][0], ready[c][1], ys[c], t)
-            neg_lam = const.tile([P, 1], F32)
-            nc.vector.tensor_scalar(
-                out=neg_lam[:], in0=exps[:, 1:2], scalar1=exps[:, 0:1], scalar2=-LAM_INIT, op0=ALU.subtract, op1=ALU.add
-            )
+            w_step = X_TILES // STEP
+            group_steps = HEADS // STEP
+            last_group = 2 * H // HEADS - 1
+            first_held = TILES - HELD
+            for n in tiles_of(0) + tiles_of(1):
+                load(n)
+            for step in range(TILES // STEP + 1):
+                for n in tiles_of(step + 2):
+                    load(n)
+                for n in tiles_of(step):
+                    turn(n)
+                done = w_tiles_of(step - 1)
+                held = bool(done) and done[0] >= first_held
+                multiplied = [(done, 0)] if held else [([n], None) for n in done]
+                for ns, v in multiplied:
+                    multiply(ns, v)
+                new = tiles_of(step)
+                b, part = divmod(step - w_step - 1 - group_steps, group_steps)
+                placing = 0 <= b
+                slots = 0 if HEADS * b + X_TILES >= first_held else None
+                if new:
+                    lift(new[0], 0, nc.scalar.copy)
+                    lift(new[0], 1, nc.vector.tensor_copy)
+                if placing:
+                    place(b, 2 * part, slots)
+                if new:
+                    lift(new[1], 0, nc.scalar.copy)
+                    lift(new[1], 1, nc.scalar.copy)
+                    quantise(new[0])
+                if placing:
+                    place(b, 2 * part + 1, slots)
+                if new:
+                    quantise(new[1])
+                for ns, v in multiplied:
+                    keep(ns, v)
+                if done and (done[-1] - X_TILES) % HEADS == HEADS - 1:
+                    cross((done[-1] - X_TILES) // HEADS, 0 if held else None)
+                if step == w_step:
+                    products = const.tile([P, 2, D], F32)
+                    nc.vector.tensor_tensor(out=products[:], in0=vectors[:, 0:2, :], in1=vectors[:, 2:4, :], op=ALU.mult)
+                    dots = const.tile([P, 2], F32)
+                    nc.vector.tensor_reduce(out=dots[:], in_=products[:], axis=AXIS_X, op=ALU.add)
+                if step == w_step + 1:
+                    nc.scalar.activation(out=exps[:], in_=dots[:], func=ACT.Exp)
+                if step == w_step + 2:
+                    nc.vector.tensor_scalar(
+                        out=neg_lam[:], in0=exps[:, 1:2], scalar1=exps[:, 0:1], scalar2=-LAM_INIT, op0=ALU.subtract, op1=ALU.add
+                    )
 
-            for n in range(4):
-                turn_heads(ys[n_chunks - 1], n, True, HEADS_PER_CHUNK * (CHUNKS_PER_W - 1))
+            pairs = [[n, n + 1] for n in range(first_held, TILES, 2)]
+            for ns in pairs:
+                multiply(ns, 1)
+            for quarter in range(4):
+                place(last_group, quarter, 0)
+            for ns in pairs:
+                keep(ns, 1)
+            late = []
+            for b in range(last_group + 1 - HELD // HEADS, last_group + 1):
+                cross(b, 1)
+                late.extend([(b, quarter) for quarter in range(4)])
 
-        with tc.tile_pool(name="soft", bufs=SOFT_STAGES + 1) as soft, tc.tile_pool(name="stats", bufs=SOFT_STAGES + 1) as stats:
             wide = [P, BATCH, HEAD_ROWS]
             banks, atts, tops, totals, inverses, moveds = {}, {}, {}, {}, {}, {}
 
             def scores(b):
-                banks[b] = sums.tile([P, BATCH, 2 * HEAD_ROWS], F32, tag="sums", name="bank")
+                pool, tag = ((turned, "turned"), (sums, "sums"))[b % 2]
+                banks[b] = pool.tile([P, BATCH, 2 * HEAD_ROWS], F32, tag=tag, name="bank")
                 for i in range(BATCH):
                     w = BATCH * b + i
                     nc.tensor.matmul(
@@ -283,3 +337,6 @@ def tile_differentialattention_pa_kernel(tc, x, Wq, Wk, lq1, lq2, lk1, lk2, out)
                 if live(r - 4):
                     divide(r - 4)
                     move_up(r - 4)
+                if 1 <= r <= len(late) // 2:
+                    for b, quarter in late[2 * r - 2 : 2 * r]:
+                        place(b, quarter, 1)

@@ -57,16 +57,24 @@ def tile_differentialattention_pa_kernel(tc, x, Wq, Wk, lq1, lq2, lk1, lk2, out)
 
         q_cols = heads.tile([P, SLOTS, 2 * HEAD_ROWS], F32)
         k_cols = heads.tile([P, SLOTS, HEAD_ROWS], F32)
-        for piece in range(16):
-            nc.gpsimd.memset(q_cols[:, 16 * piece : 16 * piece + 16, :], 0.0)
+        pieces = [q_cols[:, 16 * i : 16 * i + 16, :].rearrange("p s c -> p (s c)") for i in range(SLOTS // 16)]
+        zeros = pieces[0]
+        for i in range(3):
+            nc.vector.memset(pieces[i].bitcast(U32), 0)
+        for i in range(3, 5):
+            nc.gpsimd.memset(pieces[i].bitcast(U32), 0)
+        for i in range(5, 7):
+            nc.scalar.copy(out=pieces[i], in_=zeros)
+        by_scalar = {1: pieces[7], 2: pieces[8]}
+        by_dma = {4 + i: pieces[9 + i] for i in range(7)}
 
         vectors = const.tile([P, 4, D], BF16)
-        for i, vec in enumerate((lq1, lq2, lk1, lk2)):
-            nc.scalar.dma_start(out=vectors[:, i, :], in_=vec.partition_broadcast(P))
+        products = const.tile([P, 2, D], F32)
+        dots = const.tile([P, 2], F32)
         exps = const.tile([P, 2], F32)
         neg_lam = const.tile([P, 1], F32)
 
-        with tc.tile_pool(name="raw", bufs=3 * STEP) as raw_pool, tc.tile_pool(
+        with tc.tile_pool(name="raw", bufs=3 * STEP) as raw_pool, tc.tile_pool(name="parted", bufs=2 * STEP) as parted_pool, tc.tile_pool(
             name="grouped", bufs=2 * STEP
         ) as grouped_pool, tc.tile_pool(name="wq", bufs=HELD + STEP) as w_pool, tc.tile_pool(
             name="xq", bufs=1
@@ -75,7 +83,7 @@ def tile_differentialattention_pa_kernel(tc, x, Wq, Wk, lq1, lq2, lk1, lk2, out)
         ) as stats:
             x_codes = x_pool.tile([P, PASSES, TOKENS], U32, align_bytes=64)
             x_scales = x_pool.tile([P, PASSES, TOKENS], U8, align_bytes=64)
-            raws, turneds, groupeds, codes, accs, kepts, crossed = {}, {}, {}, {}, {}, {}, {}
+            raws, parteds, turneds, groupeds, codes, accs, kepts, crossed = {}, {}, {}, {}, {}, {}, {}, {}
 
             def load(n):
                 raws[n] = raw_pool.tile([P, C], BF16, tag="raw", name="raw")
@@ -86,26 +94,29 @@ def tile_differentialattention_pa_kernel(tc, x, Wq, Wk, lq1, lq2, lk1, lk2, out)
                     rows = (Wk, Wq)[i // H][P * (i % H) : P * (i % H) + P, :]
                 nc.sync.dma_start(out=raws[n][:], in_=rows)
 
+            def part(n):
+                parteds[n] = parted_pool.tile([P, 2, PASSES * WORDS], F32, tag="parted", name="parted")
+                nc.vector.tensor_copy(out=parteds[n][:], in_=raws[n][:].bitcast(F32).rearrange("p (w u) -> p u w", u=2))
+
             def turn(n):
-                words = raws[n][:].bitcast(F32)
                 turneds[n] = []
                 for pair in range(PASSES // 2):
                     bank = turned.tile([P, 2, 2, P], F32, tag="turned", name="turned_bank")
                     for g in range(2):
                         for u in range(2):
-                            first = 2 * WORDS * (2 * pair + g) + u
+                            first = WORDS * (2 * pair + g)
                             nc.tensor.transpose(
                                 out=bank[:, g, u, :],
-                                in_=words[:, first : first + 2 * WORDS - 1 : 2],
+                                in_=parteds[n][:, u, first : first + WORDS],
                                 identity=(ident if n < X_TILES else by_half)[:],
                             )
                     turneds[n].append(bank)
 
-            def lift(n, pair, copy):
+            def lift(n, pair):
                 if pair == 0:
                     groupeds[n] = grouped_pool.tile([P, PASSES, PACK * P], BF16, align_bytes=64, tag="grouped", name="grouped")
                 grouped_words = groupeds[n][:].bitcast(F32).rearrange("p g (o u) -> p g o u", u=2)
-                copy(
+                nc.scalar.copy(
                     out=grouped_words[:, 2 * pair : 2 * pair + 2], in_=turneds[n][pair][:].rearrange("p g u o -> p g o u")
                 )
 
@@ -191,9 +202,13 @@ def tile_differentialattention_pa_kernel(tc, x, Wq, Wk, lq1, lq2, lk1, lk2, out)
             first_held = TILES - HELD
             for n in tiles_of(0) + tiles_of(1):
                 load(n)
+            for n in tiles_of(0):
+                part(n)
             for step in range(TILES // STEP + 1):
                 for n in tiles_of(step + 2):
                     load(n)
+                if step in by_dma:
+                    nc.sync.dma_start(out=by_dma[step], in_=zeros)
                 for n in tiles_of(step):
                     turn(n)
                 done = w_tiles_of(step - 1)
@@ -202,37 +217,28 @@ def tile_differentialattention_pa_kernel(tc, x, Wq, Wk, lq1, lq2, lk1, lk2, out)
                 for ns, v in multiplied:
                     multiply(ns, v)
                 new = tiles_of(step)
-                b, part = divmod(step - w_step - 1 - group_steps, group_steps)
+                b, half = divmod(step - w_step - 1 - group_steps, group_steps)
                 placing = 0 <= b
                 slots = 0 if HEADS * b + X_TILES >= first_held else None
-                if new:
-                    lift(new[0], 0, nc.scalar.copy)
-                    lift(new[0], 1, nc.vector.tensor_copy)
-                if placing:
-                    place(b, 2 * part, slots)
-                if new:
-                    lift(new[1], 0, nc.scalar.copy)
-                    lift(new[1], 1, nc.scalar.copy)
-                    quantise(new[0])
-                if placing:
-                    place(b, 2 * part + 1, slots)
-                if new:
-                    quantise(new[1])
+                coming = tiles_of(step + 1)
+                for n in new:
+                    for pair in range(2):
+                        lift(n, pair)
+                if step in by_scalar:
+                    nc.scalar.copy(out=by_scalar[step], in_=zeros)
+                for i in range(STEP):
+                    if coming:
+                        part(coming[i])
+                    if placing:
+                        place(b, 2 * half + i, slots)
+                    if new:
+                        quantise(new[i])
                 for ns, v in multiplied:
                     keep(ns, v)
                 if done and (done[-1] - X_TILES) % HEADS == HEADS - 1:
                     cross((done[-1] - X_TILES) // HEADS, 0 if held else None)
-                if step == w_step:
-                    products = const.tile([P, 2, D], F32)
-                    nc.vector.tensor_tensor(out=products[:], in0=vectors[:, 0:2, :], in1=vectors[:, 2:4, :], op=ALU.mult)
-                    dots = const.tile([P, 2], F32)
-                    nc.vector.tensor_reduce(out=dots[:], in_=products[:], axis=AXIS_X, op=ALU.add)
-                if step == w_step + 1:
-                    nc.scalar.activation(out=exps[:], in_=dots[:], func=ACT.Exp)
-                if step == w_step + 2:
-                    nc.vector.tensor_scalar(
-                        out=neg_lam[:], in0=exps[:, 1:2], scalar1=exps[:, 0:1], scalar2=-LAM_INIT, op0=ALU.subtract, op1=ALU.add
-                    )
+            for i, vec in enumerate((lq1, lq2, lk1, lk2)):
+                nc.sync.dma_start(out=vectors[:, i, :], in_=vec.partition_broadcast(P))
 
             pairs = [[n, n + 1] for n in range(first_held, TILES, 2)]
             for ns in pairs:
@@ -314,6 +320,22 @@ def tile_differentialattention_pa_kernel(tc, x, Wq, Wk, lq1, lq2, lk1, lk2, out)
                     )
                     nc.sync.dma_start(out=out_rows[u][:, BATCH * b : BATCH * (b + 1), :], in_=result[rows])
 
+            def lam_products():
+                nc.vector.tensor_tensor(out=products[:], in0=vectors[:, 0:2, :], in1=vectors[:, 2:4, :], op=ALU.mult)
+
+            def lam_dots():
+                nc.vector.tensor_reduce(out=dots[:], in_=products[:], axis=AXIS_X, op=ALU.add)
+
+            def lam_exps():
+                nc.scalar.activation(out=exps[:], in_=dots[:], func=ACT.Exp)
+
+            def lam_negative():
+                nc.vector.tensor_scalar(
+                    out=neg_lam[:], in0=exps[:, 1:2], scalar1=exps[:, 0:1], scalar2=-LAM_INIT, op0=ALU.subtract, op1=ALU.add
+                )
+
+            lam_steps = {2: lam_products, 3: lam_dots, 4: lam_exps, 5: lam_negative}
+
             def live(b):
                 return 0 <= b < BATCHES
 
@@ -337,6 +359,8 @@ def tile_differentialattention_pa_kernel(tc, x, Wq, Wk, lq1, lq2, lk1, lk2, out)
                 if live(r - 4):
                     divide(r - 4)
                     move_up(r - 4)
+                if r in lam_steps:
+                    lam_steps[r]()
                 if 1 <= r <= len(late) // 2:
                     for b, quarter in late[2 * r - 2 : 2 * r]:
                         place(b, quarter, 1)

@@ -59,14 +59,12 @@ def tile_differentialattention_pa_kernel(tc, x, Wq, Wk, lq1, lq2, lk1, lk2, out)
         k_cols = heads.tile([P, SLOTS, HEAD_ROWS], F32)
         pieces = [q_cols[:, 16 * i : 16 * i + 16, :].rearrange("p s c -> p (s c)") for i in range(SLOTS // 16)]
         zeros = pieces[0]
-        for i in range(3):
-            nc.vector.memset(pieces[i].bitcast(U32), 0)
-        for i in range(3, 5):
+        nc.vector.memset(zeros.bitcast(U32), 0)
+        for i in range(1, 3):
             nc.gpsimd.memset(pieces[i].bitcast(U32), 0)
-        for i in range(5, 7):
-            nc.scalar.copy(out=pieces[i], in_=zeros)
-        by_scalar = {1: pieces[7], 2: pieces[8]}
-        by_dma = {4 + i: pieces[9 + i] for i in range(7)}
+        nc.scalar.copy(out=pieces[3], in_=zeros)
+        by_scalar = {1 + i: pieces[4 + i] for i in range(3)}
+        by_dma = {3 + i: pieces[7 + i] for i in range(9)}
 
         vectors = const.tile([P, 4, D], BF16)
         products = const.tile([P, 2, D], F32)
@@ -96,7 +94,10 @@ def tile_differentialattention_pa_kernel(tc, x, Wq, Wk, lq1, lq2, lk1, lk2, out)
 
             def part(n):
                 parteds[n] = parted_pool.tile([P, 2, PASSES * WORDS], F32, tag="parted", name="parted")
-                nc.vector.tensor_copy(out=parteds[n][:], in_=raws[n][:].bitcast(F32).rearrange("p (w u) -> p u w", u=2))
+                nc.vector.tensor_copy(
+                    out=parteds[n][:].rearrange("p u (b r) -> p u b r", r=8),
+                    in_=raws[n][:].bitcast(F32).rearrange("p (b u r) -> p u b r", u=2, r=8),
+                )
 
             def turn(n):
                 turneds[n] = []

@@ -107,7 +107,7 @@ def tile_differentialattention_pa_kernel(tc, x, Wq, Wk, lq1, lq2, lk1, lk2, out)
                         for u in range(2):
                             first = WORDS * (2 * pair + g)
                             nc.tensor.transpose(
-                                out=bank[:, g, u, :],
+                                out=bank[:, u, g, :],
                                 in_=parteds[n][:, u, first : first + WORDS],
                                 identity=(ident if n < X_TILES else by_half)[:],
                             )
@@ -116,9 +116,10 @@ def tile_differentialattention_pa_kernel(tc, x, Wq, Wk, lq1, lq2, lk1, lk2, out)
             def lift(n, pair):
                 if pair == 0:
                     groupeds[n] = grouped_pool.tile([P, PASSES, PACK * P], BF16, align_bytes=64, tag="grouped", name="grouped")
-                grouped_words = groupeds[n][:].bitcast(F32).rearrange("p g (o u) -> p g o u", u=2)
+                grouped_words = groupeds[n][:].bitcast(F32)[:, 2 * pair : 2 * pair + 2, :]
                 nc.scalar.copy(
-                    out=grouped_words[:, 2 * pair : 2 * pair + 2], in_=turneds[n][pair][:].rearrange("p g u o -> p g o u")
+                    out=grouped_words.rearrange("p g (o i u) -> p (g o) u i", i=2, u=2),
+                    in_=turneds[n][pair][:].rearrange("p u g (o i) -> p (g o) u i", i=2),
                 )
 
             def quantise(n):

@@ -28,6 +28,7 @@ X_TILES = TOKENS // P
 TILES = X_TILES + 2 * H
 HEADS = 4
 STEP = 2
+AHEAD = 3
 HELD = 2 * HEADS
 GROUPS = SLOTS // 2
 BATCH = 8
@@ -64,7 +65,7 @@ def tile_differentialattention_pa_kernel(tc, x, Wq, Wk, lq1, lq2, lk1, lk2, out)
             nc.gpsimd.memset(pieces[i].bitcast(U32), 0)
         nc.scalar.copy(out=pieces[3], in_=zeros)
         by_scalar = {1 + i: pieces[4 + i] for i in range(3)}
-        by_dma = {3 + i: pieces[7 + i] for i in range(9)}
+        by_vector = {3 + i: pieces[7 + i] for i in range(9)}
 
         vectors = const.tile([P, 4, D], BF16)
         products = const.tile([P, 2, D], F32)
@@ -72,8 +73,8 @@ def tile_differentialattention_pa_kernel(tc, x, Wq, Wk, lq1, lq2, lk1, lk2, out)
         exps = const.tile([P, 2], F32)
         neg_lam = const.tile([P, 1], F32)
 
-        with tc.tile_pool(name="raw", bufs=3 * STEP) as raw_pool, tc.tile_pool(name="parted", bufs=2 * STEP) as parted_pool, tc.tile_pool(
-            name="grouped", bufs=2 * STEP
+        with tc.tile_pool(name="raw", bufs=(AHEAD + 1) * STEP) as raw_pool, tc.tile_pool(name="parted", bufs=STEP + 1) as parted_pool, tc.tile_pool(
+            name="grouped", bufs=STEP + 1
         ) as grouped_pool, tc.tile_pool(name="wq", bufs=HELD + STEP) as w_pool, tc.tile_pool(
             name="xq", bufs=1
         ) as x_pool, tc.tile_pool(name="y", bufs=2) as y_pool, tc.tile_pool(name="soft", bufs=SOFT_STAGES + 1) as soft, tc.tile_pool(
@@ -171,7 +172,7 @@ def tile_differentialattention_pa_kernel(tc, x, Wq, Wk, lq1, lq2, lk1, lk2, out)
                 for t in range(2):
                     to = slice(D * t, D * t + D)
                     come = slice(D * (1 - t), D * (1 - t) + D)
-                    nc.sync.dma_start(out=crossed[b][to, :, halves(v)], in_=kepts[b][come, :, halves(v), t, :])
+                    nc.scalar.dma_start(out=crossed[b][to, :, halves(v)], in_=kepts[b][come, :, halves(v), t, :])
 
             def place(b, quarter, v):
                 t = quarter % 2
@@ -202,15 +203,13 @@ def tile_differentialattention_pa_kernel(tc, x, Wq, Wk, lq1, lq2, lk1, lk2, out)
             group_steps = HEADS // STEP
             last_group = 2 * H // HEADS - 1
             first_held = TILES - HELD
-            for n in tiles_of(0) + tiles_of(1):
+            for n in range(AHEAD * STEP):
                 load(n)
             for n in tiles_of(0):
                 part(n)
             for step in range(TILES // STEP + 1):
-                for n in tiles_of(step + 2):
+                for n in tiles_of(step + AHEAD):
                     load(n)
-                if step in by_dma:
-                    nc.sync.dma_start(out=by_dma[step], in_=zeros)
                 for n in tiles_of(step):
                     turn(n)
                 done = w_tiles_of(step - 1)
@@ -228,6 +227,8 @@ def tile_differentialattention_pa_kernel(tc, x, Wq, Wk, lq1, lq2, lk1, lk2, out)
                         lift(n, pair)
                 if step in by_scalar:
                     nc.scalar.copy(out=by_scalar[step], in_=zeros)
+                if step in by_vector:
+                    nc.vector.memset(by_vector[step].bitcast(U32), 0)
                 for i in range(STEP):
                     if coming:
                         part(coming[i])

@@ -34,6 +34,7 @@ GROUPS = SLOTS // 2
 BATCH = 8
 BATCHES = GROUPS // BATCH
 SOFT_STAGES = 7
+LAST = 5
 SCALE = D ** -0.5
 LAM_INIT = 0.8 - 0.6 * math.exp(-0.3 * 12)
 
@@ -56,16 +57,21 @@ def tile_differentialattention_pa_kernel(tc, x, Wq, Wk, lq1, lq2, lk1, lk2, out)
             out=by_half[:].rearrange("p (j d) -> p j d", j=2), in_=ident[:].rearrange("p (d j) -> p j d", j=2)
         )
 
+        shift_up = const.tile([P, 2, 2, 2 * H], F32)
+        nc.vector.memset(shift_up[:], 0.0)
+        nc.vector.tensor_copy(out=shift_up[:, :, 0, :], in_=ident[:].rearrange("p (u j r) -> p u j r", u=2, j=2)[:, :, 1, :])
+
         q_cols = heads.tile([P, SLOTS, 2 * HEAD_ROWS], F32)
         k_cols = heads.tile([P, SLOTS, HEAD_ROWS], F32)
         pieces = [q_cols[:, 16 * i : 16 * i + 16, :].rearrange("p s c -> p (s c)") for i in range(SLOTS // 16)]
         zeros = pieces[0]
-        nc.vector.memset(zeros.bitcast(U32), 0)
-        for i in range(1, 3):
+        for i in range(5):
+            nc.vector.memset(pieces[i].bitcast(U32), 0)
+        for i in range(5, 7):
             nc.gpsimd.memset(pieces[i].bitcast(U32), 0)
-        nc.scalar.copy(out=pieces[3], in_=zeros)
-        by_scalar = {1 + i: pieces[4 + i] for i in range(3)}
-        by_vector = {3 + i: pieces[7 + i] for i in range(9)}
+        nc.scalar.copy(out=pieces[7], in_=zeros)
+        by_scalar = {1 + i: pieces[8 + i] for i in range(3)}
+        by_vector = {5 + i: pieces[11 + i] for i in range(5)}
 
         vectors = const.tile([P, 4, D], BF16)
         products = const.tile([P, 2, D], F32)
@@ -93,14 +99,18 @@ def tile_differentialattention_pa_kernel(tc, x, Wq, Wk, lq1, lq2, lk1, lk2, out)
                     rows = (Wk, Wq)[i // H][P * (i % H) : P * (i % H) + P, :]
                 nc.sync.dma_start(out=raws[n][:], in_=rows)
 
+            def is_parted(n):
+                return n >= X_TILES and n % 4 != 3
+
             def part(n):
                 parteds[n] = parted_pool.tile([P, 2, PASSES * WORDS], F32, tag="parted", name="parted")
-                nc.vector.tensor_copy(
-                    out=parteds[n][:].rearrange("p u (b r) -> p u b r", r=8),
-                    in_=raws[n][:].bitcast(F32).rearrange("p (b u r) -> p u b r", u=2, r=8),
-                )
+                nc.vector.tensor_copy(out=parteds[n][:], in_=raws[n][:].bitcast(F32).rearrange("p (w u) -> p u w", u=2))
 
             def turn(n):
+                if is_parted(n):
+                    words = parteds[n][:]
+                else:
+                    words = raws[n][:].bitcast(F32).rearrange("p (w u) -> p u w", u=2)
                 turneds[n] = []
                 for pair in range(PASSES // 2):
                     bank = turned.tile([P, 2, 2, P], F32, tag="turned", name="turned_bank")
@@ -109,7 +119,7 @@ def tile_differentialattention_pa_kernel(tc, x, Wq, Wk, lq1, lq2, lk1, lk2, out)
                             first = WORDS * (2 * pair + g)
                             nc.tensor.transpose(
                                 out=bank[:, u, g, :],
-                                in_=parteds[n][:, u, first : first + WORDS],
+                                in_=words[:, u, first : first + WORDS],
                                 identity=(ident if n < X_TILES else by_half)[:],
                             )
                     turneds[n].append(bank)
@@ -156,71 +166,79 @@ def tile_differentialattention_pa_kernel(tc, x, Wq, Wk, lq1, lq2, lk1, lk2, out)
                         )
                 accs[ns[0], v] = acc
 
-            def halves(v):
-                return slice(0, 2) if v is None else slice(v, v + 1)
+            def held(b):
+                return X_TILES + HEADS * b >= first_held
+
+            def stored(b, v):
+                return ((b, v), slice(0, 1)) if held(b) else ((b, None), slice(0, 2) if v is None else slice(v, v + 1))
 
             def keep(ns, v):
                 b, h = divmod(ns[0] - X_TILES, HEADS)
-                if b not in kepts:
-                    kepts[b] = y_pool.tile([P, HEADS, 2, 2, P], F32, tag="kept", name="kept")
-                    crossed[b] = y_pool.tile([P, HEADS, 2, P], F32, tag="crossed", name="crossed")
+                key, own = stored(b, v)
+                if key not in kepts:
+                    width = 1 if held(b) else 2
+                    kepts[key] = y_pool.tile([P, HEADS, width, 2, P], F32, tag="kept", name="kept")
+                    crossed[key] = y_pool.tile([P, HEADS, width, P], F32, tag="crossed", name="crossed", bufs=3)
                 nc.scalar.copy(
-                    out=kepts[b][:, h : h + len(ns), halves(v)].rearrange("p h v t s -> p h (v t s)"), in_=accs[ns[0], v][:]
+                    out=kepts[key][:, h : h + len(ns), own].rearrange("p h v t s -> p h (v t s)"), in_=accs[ns[0], v][:]
                 )
 
             def cross(b, v):
+                key, own = stored(b, v)
                 for t in range(2):
                     to = slice(D * t, D * t + D)
                     come = slice(D * (1 - t), D * (1 - t) + D)
-                    nc.scalar.dma_start(out=crossed[b][to, :, halves(v)], in_=kepts[b][come, :, halves(v), t, :])
+                    nc.scalar.dma_start(out=crossed[key][to], in_=kepts[key][come, :, :, t, :])
 
             def place(b, quarter, v):
                 t = quarter % 2
+                key, own = stored(b, v)
+                slots = slice(0, 2) if v is None else slice(v, v + 1)
                 rows = slice(D * t, D * t + D)
                 if quarter < 2:
                     j = t
-                    source = kepts[b][rows, :, halves(v), t, :]
+                    source = kepts[key][rows, :, own, t, :]
                 else:
                     j = 1 - t
-                    source = crossed[b][rows, :, halves(v)]
+                    source = crossed[key][rows, :, own]
                 first = HEADS * (b % (H // HEADS))
                 if b < H // HEADS:
                     cols, col = k_cols, H * j + first
                 else:
                     cols, col = q_cols, 2 * H * j + H * t + first
                 nc.vector.tensor_copy(
-                    out=cols[rows, :, col : col + HEADS].rearrange("p (v s) h -> p v s h", v=2)[:, halves(v)],
+                    out=cols[rows, :, col : col + HEADS].rearrange("p (v s) h -> p v s h", v=2)[:, slots],
                     in_=source.rearrange("p h v s -> p v s h"),
                 )
 
+            first_w = list(range(X_TILES, X_TILES + HEADS))
+            order = list(range(X_TILES // 2)) + first_w + list(range(X_TILES // 2, X_TILES)) + list(range(X_TILES + HEADS, TILES))
+
             def tiles_of(step):
-                return [n for n in range(STEP * step, STEP * step + STEP) if 0 <= n < TILES]
+                return order[STEP * step : STEP * step + STEP] if step >= 0 else []
 
-            def w_tiles_of(step):
-                return [n for n in tiles_of(step) if n >= X_TILES]
-
-            w_step = X_TILES // STEP
             group_steps = HEADS // STEP
             last_group = 2 * H // HEADS - 1
             first_held = TILES - HELD
-            for n in range(AHEAD * STEP):
-                load(n)
-            for n in tiles_of(0):
-                part(n)
+            x_step = 1 + group_steps
+            for step in range(AHEAD):
+                for n in tiles_of(step):
+                    load(n)
             for step in range(TILES // STEP + 1):
                 for n in tiles_of(step + AHEAD):
                     load(n)
                 for n in tiles_of(step):
                     turn(n)
-                done = w_tiles_of(step - 1)
-                held = bool(done) and done[0] >= first_held
-                multiplied = [(done, 0)] if held else [([n], None) for n in done]
+                done = [n for n in tiles_of(step - 1) if n >= X_TILES]
+                if step == x_step + 1:
+                    multiplied = [(first_w[i : i + STEP], 1) for i in range(0, HEADS, STEP)]
+                elif done and (step <= x_step or done[0] >= first_held):
+                    multiplied = [(done, 0)]
+                else:
+                    multiplied = [([n], None) for n in done]
                 for ns, v in multiplied:
                     multiply(ns, v)
                 new = tiles_of(step)
-                b, half = divmod(step - w_step - 1 - group_steps, group_steps)
-                placing = 0 <= b
-                slots = 0 if HEADS * b + X_TILES >= first_held else None
                 coming = tiles_of(step + 1)
                 for n in new:
                     for pair in range(2):
@@ -229,25 +247,34 @@ def tile_differentialattention_pa_kernel(tc, x, Wq, Wk, lq1, lq2, lk1, lk2, out)
                     nc.scalar.copy(out=by_scalar[step], in_=zeros)
                 if step in by_vector:
                     nc.vector.memset(by_vector[step].bitcast(U32), 0)
+                b, late = divmod(step - 1 - 2 * group_steps, group_steps)
+                quarters = []
+                if late == 0 and 0 <= b <= last_group:
+                    quarters = [(b, 0), (b, 1)]
+                if late == 1 and 0 <= b - 1:
+                    quarters = [(b - 1, 2), (b - 1, 3)]
                 for i in range(STEP):
-                    if coming:
+                    if coming and is_parted(coming[i]):
                         part(coming[i])
-                    if placing:
-                        place(b, 2 * half + i, slots)
+                    if quarters:
+                        b, quarter = quarters[i]
+                        place(b, quarter, 0 if X_TILES + HEADS * b >= first_held else None)
                     if new:
                         quantise(new[i])
                 for ns, v in multiplied:
                     keep(ns, v)
-                if done and (done[-1] - X_TILES) % HEADS == HEADS - 1:
-                    cross((done[-1] - X_TILES) // HEADS, 0 if held else None)
+                if multiplied and v != 0 and (ns[-1] - X_TILES) % HEADS == HEADS - 1:
+                    cross((ns[-1] - X_TILES) // HEADS, None)
+                if done and done[0] >= first_held and (done[-1] - X_TILES) % HEADS == HEADS - 1:
+                    cross((done[-1] - X_TILES) // HEADS, 0)
             for i, vec in enumerate((lq1, lq2, lk1, lk2)):
                 nc.sync.dma_start(out=vectors[:, i, :], in_=vec.partition_broadcast(P))
 
             pairs = [[n, n + 1] for n in range(first_held, TILES, 2)]
             for ns in pairs:
                 multiply(ns, 1)
-            for quarter in range(4):
-                place(last_group, quarter, 0)
+            for b, quarter in [(last_group - 1, 2), (last_group - 1, 3)] + [(last_group, quarter) for quarter in range(4)]:
+                place(b, quarter, 0)
             for ns in pairs:
                 keep(ns, 1)
             late = []
@@ -303,6 +330,16 @@ def tile_differentialattention_pa_kernel(tc, x, Wq, Wk, lq1, lq2, lk1, lk2, out)
                 )
 
             def move_up(b):
+                if b >= BATCHES - LAST:
+                    moveds[b] = turned.tile([P, BATCH, H], F32, tag="turned", name="moved_bank")
+                    nc.tensor.matmul(
+                        out=moveds[b][:],
+                        lhsT=shift_up[:].rearrange("p u j r -> p (u j r)"),
+                        rhs=atts[b][:, :, H : 2 * H],
+                        start=True,
+                        stop=True,
+                    )
+                    return
                 moveds[b] = soft.tile([P, BATCH, H], F32, tag="moved", name="moved")
                 for u in range(2):
                     nc.sync.dma_start(
@@ -311,8 +348,8 @@ def tile_differentialattention_pa_kernel(tc, x, Wq, Wk, lq1, lq2, lk1, lk2, out)
 
             def difference(b):
                 result = soft.tile([P, BATCH, H], F32, tag="result")
-                for u in range(2):
-                    rows = slice(D * u, D * u + 2 * H)
+                halves = [slice(0, P)] if b >= BATCHES - LAST else [slice(D * u, D * u + 2 * H) for u in range(2)]
+                for rows in halves:
                     nc.vector.scalar_tensor_tensor(
                         out=result[rows],
                         in0=moveds[b][rows],
@@ -321,7 +358,10 @@ def tile_differentialattention_pa_kernel(tc, x, Wq, Wk, lq1, lq2, lk1, lk2, out)
                         op0=ALU.mult,
                         op1=ALU.add,
                     )
-                    nc.sync.dma_start(out=out_rows[u][:, BATCH * b : BATCH * (b + 1), :], in_=result[rows])
+                for u in range(2):
+                    rows = slice(D * u, D * u + 2 * H)
+                    queue = nc.scalar if u == 1 and b >= BATCHES - 2 else nc.sync
+                    queue.dma_start(out=out_rows[u][:, BATCH * b : BATCH * (b + 1), :], in_=result[rows])
 
             def lam_products():
                 nc.vector.tensor_tensor(out=products[:], in0=vectors[:, 0:2, :], in1=vectors[:, 2:4, :], op=ALU.mult)
@@ -342,7 +382,7 @@ def tile_differentialattention_pa_kernel(tc, x, Wq, Wk, lq1, lq2, lk1, lk2, out)
             def live(b):
                 return 0 <= b < BATCHES
 
-            for r in range(BATCHES + SOFT_STAGES - 1):
+            for r in range(BATCHES + 2):
                 if live(r):
                     scores(r)
                 if live(r - 1):
@@ -367,3 +407,17 @@ def tile_differentialattention_pa_kernel(tc, x, Wq, Wk, lq1, lq2, lk1, lk2, out)
                 if 1 <= r <= len(late) // 2:
                     for b, quarter in late[2 * r - 2 : 2 * r]:
                         place(b, quarter, 1)
+            before, last = BATCHES - 2, BATCHES - 1
+            exponential(last)
+            add_up(before)
+            difference(BATCHES - 4)
+            add_up(last)
+            invert(before)
+            difference(BATCHES - 3)
+            invert(last)
+            divide(before)
+            move_up(before)
+            divide(last)
+            move_up(last)
+            difference(before)
+            difference(last)

import math

import concourse.mybir as mybir
from concourse.masks import make_identity

F32 = mybir.dt.float32
BF16 = mybir.dt.bfloat16
U32 = mybir.dt.uint32
U8 = mybir.dt.uint8
FP8X4 = mybir.dt.float8_e4m3fn_x4
ALU = mybir.AluOpType
ACT = mybir.ActivationFunctionType
AXIS_X = mybir.AxisListType.X

P = 128
PACK = 4
K_PASS = P * PACK
TOKENS = 512
C = 2048
DIM = 2048
H = 16
D = 64
HEAD_ROWS = 2 * H
PASSES = C // K_PASS
WORDS = P
SLOTS = TOKENS // 2
X_TILES = TOKENS // P
TILES = X_TILES + 2 * H
HEADS = 4
STEP = 2
AHEAD = 3
HELD = 2 * HEADS
GROUPS = SLOTS // 2
BATCH = 8
BATCHES = GROUPS // BATCH
SOFT_STAGES = 7
LAST = 5
SCALE = D ** -0.5
LAM_INIT = 0.8 - 0.6 * math.exp(-0.3 * 12)

FLOPS = 2 * TOKENS * C * DIM * 2 + 2 * TOKENS * HEAD_ROWS * HEAD_ROWS * D


def tile_differentialattention_pa_kernel(tc, x, Wq, Wk, lq1, lq2, lk1, lk2, out):
    nc = tc.nc

    x_rows = x.rearrange("b n c -> (b n) c").rearrange("(v s t) c -> v t s c", v=2, t=2)
    out_rows = out.rearrange("b n a h -> (b n a) h").rearrange("(w u r) h -> u r w h", u=2, r=2 * H)

    with tc.manual_schedule(), tc.tile_pool(name="const", bufs=1) as const, tc.tile_pool(
        name="heads", bufs=1
    ) as heads, tc.psum_pool(name="turned", bufs=4) as turned, tc.psum_pool(name="sums", bufs=4) as sums:
        ident = const.tile([P, P], F32)
        make_identity(nc, ident[:])
        by_half = const.tile([P, P], F32)
        nc.vector.tensor_copy(
            out=by_half[:].rearrange("p (j d) -> p j d", j=2), in_=ident[:].rearrange("p (d j) -> p j d", j=2)
        )

        shift_up = const.tile([P, 2, 2, 2 * H], F32)
        nc.vector.memset(shift_up[:], 0.0)
        nc.vector.tensor_copy(out=shift_up[:, :, 0, :], in_=ident[:].rearrange("p (u j r) -> p u j r", u=2, j=2)[:, :, 1, :])

        q_cols = heads.tile([P, SLOTS, 2 * HEAD_ROWS], F32)
        k_cols = heads.tile([P, SLOTS, HEAD_ROWS], F32)
        pieces = [q_cols[:, 16 * i : 16 * i + 16, :].rearrange("p s c -> p (s c)") for i in range(SLOTS // 16)]
        zeros = pieces[0]
        for i in range(5):
            nc.vector.memset(pieces[i].bitcast(U32), 0)
        for i in range(5, 7):
            nc.gpsimd.memset(pieces[i].bitcast(U32), 0)
        nc.scalar.copy(out=pieces[7], in_=zeros)
        by_scalar = {1 + i: pieces[8 + i] for i in range(3)}
        by_vector = {5 + i: pieces[11 + i] for i in range(5)}

        vectors = const.tile([P, 4, D], BF16)
        products = const.tile([P, 2, D], F32)
        dots = const.tile([P, 2], F32)
        exps = const.tile([P, 2], F32)
        neg_lam = const.tile([P, 1], F32)

        with tc.tile_pool(name="raw", bufs=(AHEAD + 1) * STEP) as raw_pool, tc.tile_pool(name="parted", bufs=STEP + 1) as parted_pool, tc.tile_pool(
            name="grouped", bufs=STEP + 1
        ) as grouped_pool, tc.tile_pool(name="wq", bufs=HELD + STEP) as w_pool, tc.tile_pool(
            name="xq", bufs=1
        ) as x_pool, tc.tile_pool(name="y", bufs=2) as y_pool, tc.tile_pool(name="soft", bufs=SOFT_STAGES + 1) as soft, tc.tile_pool(
            name="stats", bufs=SOFT_STAGES + 1
        ) as stats:
            x_codes = x_pool.tile([P, PASSES, TOKENS], U32, align_bytes=64)
            x_scales = x_pool.tile([P, PASSES, TOKENS], U8, align_bytes=64)
            raws, parteds, turneds, groupeds, codes, accs, kepts, crossed = {}, {}, {}, {}, {}, {}, {}, {}

            def load(n):
                raws[n] = raw_pool.tile([P, C], BF16, tag="raw", name="raw")
                if n < X_TILES:
                    rows = x_rows[n // 2][n % 2]
                else:
                    i = n - X_TILES
                    rows = (Wk, Wq)[i // H][P * (i % H) : P * (i % H) + P, :]
                nc.sync.dma_start(out=raws[n][:], in_=rows)

            def is_parted(n):
                return n >= X_TILES and n % 4 != 3

            def part(n):
                parteds[n] = parted_pool.tile([P, 2, PASSES * WORDS], F32, tag="parted", name="parted")
                nc.vector.tensor_copy(out=parteds[n][:], in_=raws[n][:].bitcast(F32).rearrange("p (w u) -> p u w", u=2))

            def turn(n):
                if is_parted(n):
                    words = parteds[n][:]
                else:
                    words = raws[n][:].bitcast(F32).rearrange("p (w u) -> p u w", u=2)
                turneds[n] = []
                for pair in range(PASSES // 2):
                    bank = turned.tile([P, 2, 2, P], F32, tag="turned", name="turned_bank")
                    for g in range(2):
                        for u in range(2):
                            first = WORDS * (2 * pair + g)
                            nc.tensor.transpose(
                                out=bank[:, u, g, :],
                                in_=words[:, u, first : first + WORDS],
                                identity=(ident if n < X_TILES else by_half)[:],
                            )
                    turneds[n].append(bank)

            def lift(n, pair):
                if pair == 0:
                    groupeds[n] = grouped_pool.tile([P, PASSES, PACK * P], BF16, align_bytes=64, tag="grouped", name="grouped")
                grouped_words = groupeds[n][:].bitcast(F32)[:, 2 * pair : 2 * pair + 2, :]
                nc.scalar.copy(
                    out=grouped_words.rearrange("p g (o i u) -> p (g o) u i", i=2, u=2),
                    in_=turneds[n][pair][:].rearrange("p u g (o i) -> p (g o) u i", i=2),
                )

            def quantise(n):
                if n < X_TILES:
                    tokens = slice(P * n, P * n + P)
                    for g in range(PASSES):
                        nc.vector.quantize_mx(
                            out=x_codes[:, g, tokens].bitcast(FP8X4), scales=x_scales[:, g, tokens], in_=groupeds[n][:, g, :]
                        )
                else:
                    w_codes = w_pool.tile([P, PASSES * P], U32, align_bytes=64, tag="w_codes", name="w_codes")
                    w_scales = w_pool.tile([P, PASSES * P], U8, align_bytes=64, tag="w_scales", name="w_scales")
                    nc.vector.quantize_mx(
                        out=w_codes[:].bitcast(FP8X4), scales=w_scales[:], in_=groupeds[n][:].rearrange("p g w -> p (g w)")
                    )
                    codes[n] = (w_codes, w_scales)

            def multiply(ns, v):
                acc = sums.tile([P, len(ns), TOKENS // len(ns)], F32, tag="sums", name="acc")
                tokens = slice(0, TOKENS) if v is None else slice(TOKENS // 2 * v, TOKENS // 2 * (v + 1))
                for i, n in enumerate(ns):
                    w_codes, w_scales = codes[n]
                    for g in range(PASSES):
                        rows = slice(P * g, P * g + P)
                        nc.tensor.matmul_mx(
                            out=acc[:, i, :],
                            lhsT=w_codes[:, rows].bitcast(FP8X4),
                            lhsT_scale=w_scales[:, rows],
                            rhs=x_codes[:, g, tokens].bitcast(FP8X4),
                            rhs_scale=x_scales[:, g, tokens],
                            start=(g == 0),
                            stop=(g == PASSES - 1),
                        )
                accs[ns[0], v] = acc

            def held(b):
                return X_TILES + HEADS * b >= first_held

            def stored(b, v):
                return ((b, v), slice(0, 1)) if held(b) else ((b, None), slice(0, 2) if v is None else slice(v, v + 1))

            def keep(ns, v):
                b, h = divmod(ns[0] - X_TILES, HEADS)
                key, own = stored(b, v)
                if key not in kepts:
                    width = 1 if held(b) else 2
                    kepts[key] = y_pool.tile([P, HEADS, width, 2, P], F32, tag="kept", name="kept")
                    crossed[key] = y_pool.tile([P, HEADS, width, P], F32, tag="crossed", name="crossed", bufs=3)
                nc.scalar.copy(
                    out=kepts[key][:, h : h + len(ns), own].rearrange("p h v t s -> p h (v t s)"), in_=accs[ns[0], v][:]
                )

            def cross(b, v):
                key, own = stored(b, v)
                for t in range(2):
                    to = slice(D * t, D * t + D)
                    come = slice(D * (1 - t), D * (1 - t) + D)
                    nc.scalar.dma_start(out=crossed[key][to], in_=kepts[key][come, :, :, t, :])

            def place(b, quarter, v):
                t = quarter % 2
                key, own = stored(b, v)
                slots = slice(0, 2) if v is None else slice(v, v + 1)
                rows = slice(D * t, D * t + D)
                if quarter < 2:
                    j = t
                    source = kepts[key][rows, :, own, t, :]
                else:
                    j = 1 - t
                    source = crossed[key][rows, :, own]
                first = HEADS * (b % (H // HEADS))
                if b < H // HEADS:
                    cols, col = k_cols, H * j + first
                else:
                    cols, col = q_cols, 2 * H * j + H * t + first
                nc.vector.tensor_copy(
                    out=cols[rows, :, col : col + HEADS].rearrange("p (v s) h -> p v s h", v=2)[:, slots],
                    in_=source.rearrange("p h v s -> p v s h"),
                )

            first_w = list(range(X_TILES, X_TILES + HEADS))
            order = list(range(X_TILES // 2)) + first_w + list(range(X_TILES // 2, X_TILES)) + list(range(X_TILES + HEADS, TILES))

            def tiles_of(step):
                return order[STEP * step : STEP * step + STEP] if step >= 0 else []

            group_steps = HEADS // STEP
            last_group = 2 * H // HEADS - 1
            first_held = TILES - HELD
            x_step = 1 + group_steps
            for step in range(AHEAD):
                for n in tiles_of(step):
                    load(n)
            for step in range(TILES // STEP + 1):
                for n in tiles_of(step + AHEAD):
                    load(n)
                for n in tiles_of(step):
                    turn(n)
                done = [n for n in tiles_of(step - 1) if n >= X_TILES]
                if step == x_step + 1:
                    multiplied = [(first_w[i : i + STEP], 1) for i in range(0, HEADS, STEP)]
                elif done and (step <= x_step or done[0] >= first_held):
                    multiplied = [(done, 0)]
                else:
                    multiplied = [([n], None) for n in done]
                for ns, v in multiplied:
                    multiply(ns, v)
                new = tiles_of(step)
                coming = tiles_of(step + 1)
                for n in new:
                    for pair in range(2):
                        lift(n, pair)
                if step in by_scalar:
                    nc.scalar.copy(out=by_scalar[step], in_=zeros)
                if step in by_vector:
                    nc.vector.memset(by_vector[step].bitcast(U32), 0)
                b, late = divmod(step - 1 - 2 * group_steps, group_steps)
                quarters = []
                if late == 0 and 0 <= b <= last_group:
                    quarters = [(b, 0), (b, 1)]
                if late == 1 and 0 <= b - 1:
                    quarters = [(b - 1, 2), (b - 1, 3)]
                for i in range(STEP):
                    if coming and is_parted(coming[i]):
                        part(coming[i])
                    if quarters:
                        b, quarter = quarters[i]
                        place(b, quarter, 0 if X_TILES + HEADS * b >= first_held else None)
                    if new:
                        quantise(new[i])
                for ns, v in multiplied:
                    keep(ns, v)
                if multiplied and v != 0 and (ns[-1] - X_TILES) % HEADS == HEADS - 1:
                    cross((ns[-1] - X_TILES) // HEADS, None)
                if done and done[0] >= first_held and (done[-1] - X_TILES) % HEADS == HEADS - 1:
                    cross((done[-1] - X_TILES) // HEADS, 0)
            for i, vec in enumerate((lq1, lq2, lk1, lk2)):
                nc.sync.dma_start(out=vectors[:, i, :], in_=vec.partition_broadcast(P))

            pairs = [[n, n + 1] for n in range(first_held, TILES, 2)]
            for ns in pairs:
                multiply(ns, 1)
            for b, quarter in [(last_group - 1, 2), (last_group - 1, 3)] + [(last_group, quarter) for quarter in range(4)]:
                place(b, quarter, 0)
            for ns in pairs:
                keep(ns, 1)
            late = []
            for b in range(last_group + 1 - HELD // HEADS, last_group + 1):
                cross(b, 1)
                late.extend([(b, quarter) for quarter in range(4)])

            wide = [P, BATCH, HEAD_ROWS]
            banks, atts, tops, totals, inverses, moveds = {}, {}, {}, {}, {}, {}

            def scores(b):
                pool, tag = ((turned, "turned"), (sums, "sums"))[b % 2]
                banks[b] = pool.tile([P, BATCH, 2 * HEAD_ROWS], F32, tag=tag, name="bank")
                for i in range(BATCH):
                    w = BATCH * b + i
                    nc.tensor.matmul(
                        out=banks[b][:, i, :],
                        lhsT=q_cols[:, 2 * w : 2 * w + 2, :].rearrange("p s c -> p (s c)"),
                        rhs=k_cols[:, 2 * w : 2 * w + 2, :].rearrange("p s c -> p (s c)"),
                        start=True,
                        stop=True,
                    )

            def copy_scores(b):
                atts[b] = soft.tile(wide, F32, tag="att", name="att")
                for u in range(2):
                    rows = slice(D * u, D * u + D)
                    nc.scalar.copy(out=atts[b][rows], in_=banks[b][rows, :, HEAD_ROWS * u : HEAD_ROWS * (u + 1)])

            def largest(b):
                tops[b] = stats.tile([P, BATCH], F32, tag="top", name="top")
                nc.vector.tensor_reduce(out=tops[b][:], in_=atts[b][:], axis=AXIS_X, op=ALU.max)

            def shift(b):
                nc.vector.tensor_tensor(
                    out=atts[b][:], in0=atts[b][:], in1=tops[b][:].unsqueeze(2).to_broadcast(wide), op=ALU.subtract
                )

            def exponential(b):
                nc.scalar.activation(out=atts[b][:], in_=atts[b][:], func=ACT.Exp, scale=SCALE)

            def add_up(b):
                totals[b] = stats.tile([P, BATCH], F32, tag="total", name="total")
                nc.vector.tensor_reduce(out=totals[b][:], in_=atts[b][:], axis=AXIS_X, op=ALU.add)

            def invert(b):
                inverses[b] = stats.tile([P, BATCH], F32, tag="inverse", name="inverse")
                nc.vector.reciprocal(out=inverses[b][:], in_=totals[b][:])

            def divide(b):
                nc.vector.tensor_tensor(
                    out=atts[b][:], in0=atts[b][:], in1=inverses[b][:].unsqueeze(2).to_broadcast(wide), op=ALU.mult
                )

            def move_up(b):
                if b >= BATCHES - LAST:
                    moveds[b] = turned.tile([P, BATCH, H], F32, tag="turned", name="moved_bank")
                    nc.tensor.matmul(
                        out=moveds[b][:],
                        lhsT=shift_up[:].rearrange("p u j r -> p (u j r)"),
                        rhs=atts[b][:, :, H : 2 * H],
                        start=True,
                        stop=True,
                    )
                    return
                moveds[b] = soft.tile([P, BATCH, H], F32, tag="moved", name="moved")
                for u in range(2):
                    nc.sync.dma_start(
                        out=moveds[b][D * u : D * u + 2 * H], in_=atts[b][D * u + 2 * H : D * u + 4 * H, :, H : 2 * H]
                    )

            def difference(b):
                result = soft.tile([P, BATCH, H], F32, tag="result")
                halves = [slice(0, P)] if b >= BATCHES - LAST else [slice(D * u, D * u + 2 * H) for u in range(2)]
                for rows in halves:
                    nc.vector.scalar_tensor_tensor(
                        out=result[rows],
                        in0=moveds[b][rows],
                        scalar=neg_lam[rows, 0:1],
                        in1=atts[b][rows, :, 0:H],
                        op0=ALU.mult,
                        op1=ALU.add,
                    )
                for u in range(2):
                    rows = slice(D * u, D * u + 2 * H)
                    queue = nc.scalar if u == 1 and b >= BATCHES - 2 else nc.sync
                    queue.dma_start(out=out_rows[u][:, BATCH * b : BATCH * (b + 1), :], in_=result[rows])

            def lam_products():
                nc.vector.tensor_tensor(out=products[:], in0=vectors[:, 0:2, :], in1=vectors[:, 2:4, :], op=ALU.mult)

            def lam_dots():
                nc.vector.tensor_reduce(out=dots[:], in_=products[:], axis=AXIS_X, op=ALU.add)

            def lam_exps():
                nc.scalar.activation(out=exps[:], in_=dots[:], func=ACT.Exp)

            def lam_negative():
                nc.vector.tensor_scalar(
                    out=neg_lam[:], in0=exps[:, 1:2], scalar1=exps[:, 0:1], scalar2=-LAM_INIT, op0=ALU.subtract, op1=ALU.add
                )

            lam_steps = {2: lam_products, 3: lam_dots, 4: lam_exps, 5: lam_negative}

            def live(b):
                return 0 <= b < BATCHES

            for r in range(BATCHES + 2):
                if live(r):
                    scores(r)
                if live(r - 1):
                    copy_scores(r - 1)
                if live(r - 3):
                    exponential(r - 3)
                if live(r - 2):
                    largest(r - 2)
                if live(r - 4):
                    add_up(r - 4)
                if live(r - 2):
                    shift(r - 2)
                if live(r - 4):
                    invert(r - 4)
                if live(r - 6):
                    difference(r - 6)
                if live(r - 4):
                    divide(r - 4)
                    move_up(r - 4)
                if r in lam_steps:
                    lam_steps[r]()
                if 1 <= r <= len(late) // 2:
                    for b, quarter in late[2 * r - 2 : 2 * r]:
                        place(b, quarter, 1)
            before, last = BATCHES - 2, BATCHES - 1
            exponential(last)
            add_up(before)
            difference(BATCHES - 4)
            add_up(last)
            invert(before)
            difference(BATCHES - 3)
            invert(last)
            divide(before)
            move_up(before)
            divide(last)
            move_up(last)
            difference(before)
            difference(last)
